import numpy as np
import ml_dtypes

BF16 = ml_dtypes.bfloat16


def bf(x):
    return np.asarray(x, np.float32).astype(BF16)


def f32(x):
    return np.asarray(x, np.float32)


def f64(x):
    return np.asarray(x).astype(np.float64)


def striped(idx):
    return np.tile(idx.reshape(-1, 16).T, (8, 1))


C, S, N, T, P, H1, H2, H3, H4 = 1024, 2048, 1024, 4, 256, 640, 512, 384, 256


def weight(din, dout):
    return bf(np.random.standard_normal((T * din, dout)) * np.sqrt(2.0 / din))


def bias(dout):
    return f32(0.2 * np.random.standard_normal((T * dout, 1)))


def layer(h, w, b, din, dout):
    wt = f64(w).reshape(T, din, dout).transpose(0, 2, 1)
    return np.maximum(np.matmul(wt, h) + f64(b).reshape(T, dout, 1), 0.0)


def setup_inputs():
    return {"x": f32(np.random.standard_normal((C, S))), "w1": weight(P, H1), "b1": bias(H1), "w2": weight(H1, H2), "b2": bias(H2), "w3": weight(H2, H3), "b3": bias(H3), "w4": weight(H3, H4), "b4": bias(H4), "offs": striped(np.random.permutation(np.tile(np.arange(S), 2))[:N])}


def reference(x, w1, b1, w2, b2, w3, b3, w4, b4, offs):
    idx = offs[:16].T.reshape(-1)
    h = f64(x)[:, idx].T.reshape(T, P, C)
    h = layer(h, w1, b1, P, H1)
    h = layer(h, w2, b2, H1, H2)
    h = layer(h, w3, b3, H2, H3)
    h = layer(h, w4, b4, H3, H4)
    return h.reshape(T * H4, C)

@@ -1,0 +1,142 @@
+import concourse.mybir as mybir
+from concourse.masks import make_identity
+
+BF16, F32, U16 = mybir.dt.bfloat16, mybir.dt.float32, mybir.dt.uint16
+COPY = mybir.ActivationFunctionType.Copy
+RELU = mybir.ActivationFunctionType.Relu
+ADD, MAX = mybir.AluOpType.add, mybir.AluOpType.max
+
+P = 128
+SAMPLES, FEATURES, ENTRIES, TERMS = 1024, 2048, 1024, 4
+UNITS = (256, 640, 512, 384, 256)
+LAYERS = 4
+CHUNK = 512
+BLOCKS = CHUNK // P
+PAIR = 2
+PIECE = PAIR * UNITS[0]
+FLOPS = 2 * SAMPLES * TERMS * sum(UNITS[l] * UNITS[l + 1] for l in range(LAYERS))
+
+
+def tile_mlp_cutoff_b_kernel(tc, x, w1, b1, w2, b2, w3, b3, w4, b4, offs, out):
+    nc = tc.nc
+    w_dram = (w1, w2, w3, w4)
+    b_dram = (b1, b2, b3, b4)
+    k_tiles = [UNITS[l] // P for l in range(LAYERS)]
+    m_tiles = [UNITS[l + 1] // P for l in range(LAYERS)]
+    bias_base = [TERMS * sum(m_tiles[:l]) for l in range(LAYERS)]
+    bias_count = TERMS * sum(m_tiles)
+
+    with (
+        tc.tile_pool(name="held", bufs=1) as held,
+        tc.tile_pool(name="picked", bufs=BLOCKS) as picked,
+        tc.tile_pool(name="flipped", bufs=2) as flipped,
+        tc.tile_pool(name="acts", bufs=2 * PAIR) as acts,
+        tc.tile_pool(name="staged", bufs=4) as staged,
+        tc.psum_pool(name="sums", bufs=6) as sums,
+        tc.psum_pool(name="turned", bufs=2) as turned,
+    ):
+        offsets = held.tile([P, ENTRIES // 16], U16, name="offsets")
+        nc.sync.dma_start(offsets[:], offs)
+
+        bias_rows = held.tile([bias_count, P], F32, name="bias_rows")
+        for l in range(LAYERS):
+            rows = TERMS * m_tiles[l]
+            nc.sync.dma_start(
+                bias_rows[bias_base[l] : bias_base[l] + rows, :],
+                b_dram[l].rearrange("(r p) one -> r (p one)", p=P),
+            )
+
+        x_blocks = [held.tile([P, FEATURES], F32, name=f"x{b}") for b in range(SAMPLES // P)]
+        weights = [
+            [held.tile([P, k_tiles[l], UNITS[l + 1]], BF16, name=f"w{l}_{t}") for t in range(TERMS)]
+            for l in range(LAYERS)
+        ]
+
+        def load_x(chunk):
+            for b in range(chunk * BLOCKS, (chunk + 1) * BLOCKS):
+                nc.sync.dma_start(x_blocks[b][:], x[b * P : (b + 1) * P, :])
+
+        def load_weights(pair):
+            for l in range(LAYERS):
+                for t in range(pair * PAIR, (pair + 1) * PAIR):
+                    nc.sync.dma_start(
+                        weights[l][t][:],
+                        w_dram[l][t * UNITS[l] : (t + 1) * UNITS[l], :].rearrange("(k p) a -> p k a", p=P),
+                    )
+
+        load_x(0)
+        load_weights(0)
+        load_weights(1)
+        load_x(1)
+
+        ident_bf = held.tile([P, P], BF16, name="ident_bf")
+        make_identity(nc, ident_bf[:])
+        ident_f = held.tile([bias_count, bias_count], F32, name="ident_f")
+        make_identity(nc, ident_f[:])
+
+        bias_ps = sums.tile([P, CHUNK], F32, name="acc")
+        nc.tensor.transpose(bias_ps[:, :bias_count], bias_rows[:], ident_f[:])
+        bias = held.tile([P, bias_count], F32, name="bias")
+        nc.vector.tensor_copy(bias[:], bias_ps[:, :bias_count])
+
+        def gather(chunk, pair):
+            piece = offsets[:, pair * PIECE // 16 : (pair + 1) * PIECE // 16]
+            rounded = []
+            for b in range(chunk * BLOCKS, (chunk + 1) * BLOCKS):
+                xi = picked.tile([P, PIECE], F32, name="xi")
+                nc.scalar.activation(xi[:], x_blocks[b][:].indirect(piece), COPY)
+                xi_bf = picked.tile([P, PIECE], BF16, name="xi_bf")
+                nc.vector.tensor_copy(xi_bf[:], xi[:])
+                rounded.append(xi_bf)
+            return rounded
+
+        def flip(rounded):
+            xi_t = flipped.tile([P, PIECE // P, CHUNK], BF16, name="xi_t")
+            for b, xi_bf in enumerate(rounded):
+                turn = turned.tile([P, PIECE], BF16, name="turn")
+                for j in range(PIECE // P):
+                    nc.tensor.transpose(turn[:, j * P : (j + 1) * P], xi_bf[:, j * P : (j + 1) * P], ident_bf[:])
+                nc.vector.tensor_copy(
+                    xi_t[:, :, b * P : (b + 1) * P], turn[:].rearrange("p (j c) -> p j c", c=P)
+                )
+            return xi_t
+
+        def dense(l, t, chunk, moving):
+            last = l == LAYERS - 1
+            h = None if last else acts.tile([P, m_tiles[l], CHUNK], BF16, name=f"h{l}")
+            for m in range(m_tiles[l]):
+                acc = sums.tile([P, CHUNK], F32, name="acc")
+                for k in range(k_tiles[l]):
+                    nc.tensor.matmul(
+                        acc[:],
+                        weights[l][t][:, k, m * P : (m + 1) * P],
+                        moving[k],
+                        start=(k == 0),
+                        stop=(k == k_tiles[l] - 1),
+                    )
+                column = bias_base[l] + t * m_tiles[l] + m
+                y = staged.tile([P, CHUNK], F32, name="y") if last else None
+                dest = y[:] if last else h[:, m, :]
+                if m % 2 == 0:
+                    nc.vector.tensor_scalar(dest, acc[:], bias[:, column : column + 1], 0.0, ADD, MAX)
+                else:
+                    nc.scalar.activation(dest, acc[:], RELU, bias=bias[:, column : column + 1])
+                if last:
+                    row = t * UNITS[LAYERS] + m * P
+                    nc.sync.dma_start(out[row : row + P, chunk * CHUNK : (chunk + 1) * CHUNK], y[:])
+            return None if last else [h[:, m, :] for m in range(m_tiles[l])]
+
+        jobs = [(chunk, pair) for chunk in range(SAMPLES // CHUNK) for pair in range(TERMS // PAIR)]
+        xi_t = flip(gather(*jobs[0]))
+        for i, (chunk, pair) in enumerate(jobs):
+            terms = list(range(pair * PAIR, (pair + 1) * PAIR))
+            moving = {
+                t: [xi_t[:, s * k_tiles[0] + k, :] for k in range(k_tiles[0])] for s, t in enumerate(terms)
+            }
+            for l in range(LAYERS):
+                for t in terms:
+                    moving[t] = dense(l, t, chunk, moving[t])
+                if i + 1 < len(jobs) and l == 0:
+                    rounded = gather(*jobs[i + 1])
+                if i + 1 < len(jobs) and l == 1:
+                    xi_t = flip(rounded)

@@ -10,8 +10,8 @@ P = 128
 SAMPLES, FEATURES, ENTRIES, TERMS = 1024, 2048, 1024, 4
 UNITS = (256, 640, 512, 384, 256)
 LAYERS = 4
-CHUNK = 512
-BLOCKS = CHUNK // P
+CHUNKS = (256, 256, 512)
+TURN = 256
 PAIR = 2
 PIECE = PAIR * UNITS[0]
 FLOPS = 2 * SAMPLES * TERMS * sum(UNITS[l] * UNITS[l + 1] for l in range(LAYERS))
@@ -28,7 +28,7 @@ def tile_mlp_cutoff_b_kernel(tc, x, w1, b1, w2, b2, w3, b3, w4, b4, offs, out):
 
     with (
         tc.tile_pool(name="held", bufs=1) as held,
-        tc.tile_pool(name="picked", bufs=BLOCKS) as picked,
+        tc.tile_pool(name="picked", bufs=max(CHUNKS) // P) as picked,
         tc.tile_pool(name="flipped", bufs=2) as flipped,
         tc.tile_pool(name="acts", bufs=2 * PAIR) as acts,
         tc.tile_pool(name="staged", bufs=4) as staged,
@@ -52,8 +52,8 @@ def tile_mlp_cutoff_b_kernel(tc, x, w1, b1, w2, b2, w3, b3, w4, b4, offs, out):
             for l in range(LAYERS)
         ]
 
-        def load_x(chunk):
-            for b in range(chunk * BLOCKS, (chunk + 1) * BLOCKS):
+        def load_x(first, count):
+            for b in range(first, first + count):
                 nc.sync.dma_start(x_blocks[b][:], x[b * P : (b + 1) * P, :])
 
         def load_weights(pair):
@@ -64,25 +64,25 @@ def tile_mlp_cutoff_b_kernel(tc, x, w1, b1, w2, b2, w3, b3, w4, b4, offs, out):
                         w_dram[l][t * UNITS[l] : (t + 1) * UNITS[l], :].rearrange("(k p) a -> p k a", p=P),
                     )
 
-        load_x(0)
+        load_x(0, CHUNKS[0] // P)
         load_weights(0)
         load_weights(1)
-        load_x(1)
+        load_x(CHUNKS[0] // P, (SAMPLES - CHUNKS[0]) // P)
 
         ident_bf = held.tile([P, P], BF16, name="ident_bf")
         make_identity(nc, ident_bf[:])
         ident_f = held.tile([bias_count, bias_count], F32, name="ident_f")
         make_identity(nc, ident_f[:])
 
-        bias_ps = sums.tile([P, CHUNK], F32, name="acc")
-        nc.tensor.transpose(bias_ps[:, :bias_count], bias_rows[:], ident_f[:])
+        bias_ps = sums.tile([P, bias_count], F32, name="acc")
+        nc.tensor.transpose(bias_ps[:], bias_rows[:], ident_f[:])
         bias = held.tile([P, bias_count], F32, name="bias")
-        nc.vector.tensor_copy(bias[:], bias_ps[:, :bias_count])
+        nc.vector.tensor_copy(bias[:], bias_ps[:])
 
-        def gather(chunk, pair):
+        def gather(start, width, pair):
             piece = offsets[:, pair * PIECE // 16 : (pair + 1) * PIECE // 16]
             rounded = []
-            for b in range(chunk * BLOCKS, (chunk + 1) * BLOCKS):
+            for b in range(start // P, (start + width) // P):
                 xi = picked.tile([P, PIECE], F32, name="xi")
                 nc.scalar.activation(xi[:], x_blocks[b][:].indirect(piece), COPY)
                 xi_bf = picked.tile([P, PIECE], BF16, name="xi_bf")
@@ -91,21 +91,23 @@ def tile_mlp_cutoff_b_kernel(tc, x, w1, b1, w2, b2, w3, b3, w4, b4, offs, out):
             return rounded
 
         def flip(rounded):
-            xi_t = flipped.tile([P, PIECE // P, CHUNK], BF16, name="xi_t")
-            for b, xi_bf in enumerate(rounded):
-                turn = turned.tile([P, PIECE], BF16, name="turn")
-                for j in range(PIECE // P):
-                    nc.tensor.transpose(turn[:, j * P : (j + 1) * P], xi_bf[:, j * P : (j + 1) * P], ident_bf[:])
-                nc.vector.tensor_copy(
-                    xi_t[:, :, b * P : (b + 1) * P], turn[:].rearrange("p (j c) -> p j c", c=P)
-                )
+            xi_t = flipped.tile([P, PIECE // P, len(rounded) * P], BF16, name="xi_t")
+            for g in range(len(rounded) * P // TURN):
+                turn = turned.tile([P, PIECE // P, TURN], BF16, name="turn")
+                for s in range(TURN // P):
+                    xi_bf = rounded[g * TURN // P + s]
+                    for j in range(PIECE // P):
+                        nc.tensor.transpose(
+                            turn[:, j, s * P : (s + 1) * P], xi_bf[:, j * P : (j + 1) * P], ident_bf[:]
+                        )
+                nc.vector.tensor_copy(xi_t[:, :, g * TURN : (g + 1) * TURN], turn[:])
             return xi_t
 
-        def dense(l, t, chunk, moving):
+        def dense(l, t, start, width, moving):
             last = l == LAYERS - 1
-            h = None if last else acts.tile([P, m_tiles[l], CHUNK], BF16, name=f"h{l}")
+            h = None if last else acts.tile([P, m_tiles[l], width], BF16, name=f"h{l}")
             for m in range(m_tiles[l]):
-                acc = sums.tile([P, CHUNK], F32, name="acc")
+                acc = sums.tile([P, width], F32, name="acc")
                 for k in range(k_tiles[l]):
                     nc.tensor.matmul(
                         acc[:],
@@ -115,7 +117,7 @@ def tile_mlp_cutoff_b_kernel(tc, x, w1, b1, w2, b2, w3, b3, w4, b4, offs, out):
                         stop=(k == k_tiles[l] - 1),
                     )
                 column = bias_base[l] + t * m_tiles[l] + m
-                y = staged.tile([P, CHUNK], F32, name="y") if last else None
+                y = staged.tile([P, width], F32, name="y") if last else None
                 dest = y[:] if last else h[:, m, :]
                 if m % 2 == 0:
                     nc.vector.tensor_scalar(dest, acc[:], bias[:, column : column + 1], 0.0, ADD, MAX)
@@ -123,19 +125,21 @@ def tile_mlp_cutoff_b_kernel(tc, x, w1, b1, w2, b2, w3, b3, w4, b4, offs, out):
                     nc.scalar.activation(dest, acc[:], RELU, bias=bias[:, column : column + 1])
                 if last:
                     row = t * UNITS[LAYERS] + m * P
-                    nc.sync.dma_start(out[row : row + P, chunk * CHUNK : (chunk + 1) * CHUNK], y[:])
+                    nc.sync.dma_start(out[row : row + P, start : start + width], y[:])
             return None if last else [h[:, m, :] for m in range(m_tiles[l])]
 
-        jobs = [(chunk, pair) for chunk in range(SAMPLES // CHUNK) for pair in range(TERMS // PAIR)]
+        jobs = [
+            (sum(CHUNKS[:c]), CHUNKS[c], pair) for c in range(len(CHUNKS)) for pair in range(TERMS // PAIR)
+        ]
         xi_t = flip(gather(*jobs[0]))
-        for i, (chunk, pair) in enumerate(jobs):
+        for i, (start, width, pair) in enumerate(jobs):
             terms = list(range(pair * PAIR, (pair + 1) * PAIR))
             moving = {
                 t: [xi_t[:, s * k_tiles[0] + k, :] for k in range(k_tiles[0])] for s, t in enumerate(terms)
             }
             for l in range(LAYERS):
                 for t in terms:
-                    moving[t] = dense(l, t, chunk, moving[t])
+                    moving[t] = dense(l, t, start, width, moving[t])
                 if i + 1 < len(jobs) and l == 0:
                     rounded = gather(*jobs[i + 1])
                 if i + 1 < len(jobs) and l == 1:

@@ -11,9 +11,7 @@ SAMPLES, FEATURES, ENTRIES, TERMS = 1024, 2048, 1024, 4
 UNITS = (256, 640, 512, 384, 256)
 LAYERS = 4
 CHUNKS = (256, 256, 512)
-TURN = 256
 PAIR = 2
-PIECE = PAIR * UNITS[0]
 FLOPS = 2 * SAMPLES * TERMS * sum(UNITS[l] * UNITS[l + 1] for l in range(LAYERS))
 
 
@@ -28,8 +26,8 @@ def tile_mlp_cutoff_b_kernel(tc, x, w1, b1, w2, b2, w3, b3, w4, b4, offs, out):
 
     with (
         tc.tile_pool(name="held", bufs=1) as held,
-        tc.tile_pool(name="picked", bufs=max(CHUNKS) // P) as picked,
-        tc.tile_pool(name="flipped", bufs=2) as flipped,
+        tc.tile_pool(name="picked", bufs=PAIR * max(CHUNKS) // P) as picked,
+        tc.tile_pool(name="flipped", bufs=2 * PAIR) as flipped,
         tc.tile_pool(name="acts", bufs=2 * PAIR) as acts,
         tc.tile_pool(name="staged", bufs=4) as staged,
         tc.psum_pool(name="sums", bufs=6) as sums,
@@ -37,14 +35,6 @@ def tile_mlp_cutoff_b_kernel(tc, x, w1, b1, w2, b2, w3, b3, w4, b4, offs, out):
     ):
         offsets = held.tile([P, ENTRIES // 16], U16, name="offsets")
         nc.sync.dma_start(offsets[:], offs)
-
-        bias_rows = held.tile([bias_count, P], F32, name="bias_rows")
-        for l in range(LAYERS):
-            rows = TERMS * m_tiles[l]
-            nc.sync.dma_start(
-                bias_rows[bias_base[l] : bias_base[l] + rows, :],
-                b_dram[l].rearrange("(r p) one -> r (p one)", p=P),
-            )
 
         x_blocks = [held.tile([P, FEATURES], F32, name=f"x{b}") for b in range(SAMPLES // P)]
         weights = [
@@ -69,39 +59,45 @@ def tile_mlp_cutoff_b_kernel(tc, x, w1, b1, w2, b2, w3, b3, w4, b4, offs, out):
         load_weights(1)
         load_x(CHUNKS[0] // P, (SAMPLES - CHUNKS[0]) // P)
 
-        ident_bf = held.tile([P, P], BF16, name="ident_bf")
-        make_identity(nc, ident_bf[:])
-        ident_f = held.tile([bias_count, bias_count], F32, name="ident_f")
+        bias_rows = held.tile([bias_count, P], F32, name="bias_rows")
+        for l in range(LAYERS):
+            rows = TERMS * m_tiles[l]
+            nc.scalar.dma_start(
+                bias_rows[bias_base[l] : bias_base[l] + rows, :],
+                b_dram[l].rearrange("(r p) one -> r (p one)", p=P),
+            )
+
+        ident_f = held.tile([P, P], F32, name="ident_f")
         make_identity(nc, ident_f[:])
+        ident_bf = held.tile([P, P], BF16, name="ident_bf")
+        nc.scalar.activation(ident_bf[:], ident_f[:], COPY)
 
         bias_ps = sums.tile([P, bias_count], F32, name="acc")
-        nc.tensor.transpose(bias_ps[:], bias_rows[:], ident_f[:])
+        nc.tensor.transpose(bias_ps[:], bias_rows[:], ident_f[:bias_count, :bias_count])
         bias = held.tile([P, bias_count], F32, name="bias")
         nc.vector.tensor_copy(bias[:], bias_ps[:])
 
-        def gather(start, width, pair):
-            piece = offsets[:, pair * PIECE // 16 : (pair + 1) * PIECE // 16]
-            rounded = []
+        def gather(start, width, terms):
+            rounded = {t: [] for t in terms}
             for b in range(start // P, (start + width) // P):
-                xi = picked.tile([P, PIECE], F32, name="xi")
-                nc.scalar.activation(xi[:], x_blocks[b][:].indirect(piece), COPY)
-                xi_bf = picked.tile([P, PIECE], BF16, name="xi_bf")
-                nc.vector.tensor_copy(xi_bf[:], xi[:])
-                rounded.append(xi_bf)
+                for t in terms:
+                    piece = offsets[:, t * UNITS[0] // 16 : (t + 1) * UNITS[0] // 16]
+                    xi = picked.tile([P, UNITS[0]], F32, name="xi")
+                    nc.scalar.activation(xi[:], x_blocks[b][:].indirect(piece), COPY)
+                    xi_bf = picked.tile([P, UNITS[0]], BF16, name="xi_bf")
+                    nc.vector.tensor_copy(xi_bf[:], xi[:])
+                    rounded[t].append(xi_bf)
             return rounded
 
-        def flip(rounded):
-            xi_t = flipped.tile([P, PIECE // P, len(rounded) * P], BF16, name="xi_t")
-            for g in range(len(rounded) * P // TURN):
-                turn = turned.tile([P, PIECE // P, TURN], BF16, name="turn")
-                for s in range(TURN // P):
-                    xi_bf = rounded[g * TURN // P + s]
-                    for j in range(PIECE // P):
-                        nc.tensor.transpose(
-                            turn[:, j, s * P : (s + 1) * P], xi_bf[:, j * P : (j + 1) * P], ident_bf[:]
-                        )
-                nc.vector.tensor_copy(xi_t[:, :, g * TURN : (g + 1) * TURN], turn[:])
-            return xi_t
+        def flip(blocks):
+            width = len(blocks) * P
+            turn = turned.tile([P, k_tiles[0], width], BF16, name="turn")
+            for s, xi_bf in enumerate(blocks):
+                for k in range(k_tiles[0]):
+                    nc.tensor.transpose(turn[:, k, s * P : (s + 1) * P], xi_bf[:, k * P : (k + 1) * P], ident_bf[:])
+            xi_t = flipped.tile([P, k_tiles[0], width], BF16, name="xi_t")
+            nc.vector.tensor_copy(xi_t[:], turn[:])
+            return [xi_t[:, k, :] for k in range(k_tiles[0])]
 
         def dense(l, t, start, width, moving):
             last = l == LAYERS - 1
@@ -129,18 +125,17 @@ def tile_mlp_cutoff_b_kernel(tc, x, w1, b1, w2, b2, w3, b3, w4, b4, offs, out):
             return None if last else [h[:, m, :] for m in range(m_tiles[l])]
 
         jobs = [
-            (sum(CHUNKS[:c]), CHUNKS[c], pair) for c in range(len(CHUNKS)) for pair in range(TERMS // PAIR)
+            (sum(CHUNKS[:c]), CHUNKS[c], tuple(range(first, first + PAIR)))
+            for c in range(len(CHUNKS))
+            for first in range(0, TERMS, PAIR)
         ]
-        xi_t = flip(gather(*jobs[0]))
-        for i, (start, width, pair) in enumerate(jobs):
-            terms = list(range(pair * PAIR, (pair + 1) * PAIR))
-            moving = {
-                t: [xi_t[:, s * k_tiles[0] + k, :] for k in range(k_tiles[0])] for s, t in enumerate(terms)
-            }
+        moving = {t: flip(blocks) for t, blocks in gather(*jobs[0]).items()}
+        for i, (start, width, terms) in enumerate(jobs):
             for l in range(LAYERS):
                 for t in terms:
                     moving[t] = dense(l, t, start, width, moving[t])
                 if i + 1 < len(jobs) and l == 0:
                     rounded = gather(*jobs[i + 1])
                 if i + 1 < len(jobs) and l == 1:
-                    xi_t = flip(rounded)
+                    for t, blocks in rounded.items():
+                        moving[t] = flip(blocks)

@@ -54,26 +54,31 @@ def tile_mlp_cutoff_b_kernel(tc, x, w1, b1, w2, b2, w3, b3, w4, b4, offs, out):
                         w_dram[l][t * UNITS[l] : (t + 1) * UNITS[l], :].rearrange("(k p) a -> p k a", p=P),
                     )
 
-        load_x(0, CHUNKS[0] // P)
+        load_x(0, 1)
+        bias_rows = held.tile([bias_count, P], F32, name="bias_rows")
+        for l in range(LAYERS):
+            rows = TERMS * m_tiles[l]
+            nc.sync.dma_start(
+                bias_rows[bias_base[l] : bias_base[l] + rows, :],
+                b_dram[l].rearrange("(r p) one -> r (p one)", p=P),
+            )
+        load_x(1, CHUNKS[0] // P - 1)
         load_weights(0)
         load_weights(1)
         load_x(CHUNKS[0] // P, (SAMPLES - CHUNKS[0]) // P)
 
-        bias_rows = held.tile([bias_count, P], F32, name="bias_rows")
-        for l in range(LAYERS):
-            rows = TERMS * m_tiles[l]
-            nc.scalar.dma_start(
-                bias_rows[bias_base[l] : bias_base[l] + rows, :],
-                b_dram[l].rearrange("(r p) one -> r (p one)", p=P),
-            )
+        zeros = held.tile([P, 1], F32, name="zeros")
+        nc.vector.memset(zeros[:], 0.0)
+        primed = held.tile([P, 1], F32, name="primed")
+        nc.scalar.activation(primed[:], zeros[:], COPY)
 
-        ident_f = held.tile([P, P], F32, name="ident_f")
-        make_identity(nc, ident_f[:])
         ident_bf = held.tile([P, P], BF16, name="ident_bf")
-        nc.scalar.activation(ident_bf[:], ident_f[:], COPY)
+        make_identity(nc, ident_bf[:])
+        ident_f = held.tile([bias_count, bias_count], F32, name="ident_f")
+        make_identity(nc, ident_f[:])
 
         bias_ps = sums.tile([P, bias_count], F32, name="acc")
-        nc.tensor.transpose(bias_ps[:], bias_rows[:], ident_f[:bias_count, :bias_count])
+        nc.tensor.transpose(bias_ps[:], bias_rows[:], ident_f[:])
         bias = held.tile([P, bias_count], F32, name="bias")
         nc.vector.tensor_copy(bias[:], bias_ps[:])
 

@@ -12,6 +12,9 @@ UNITS = (256, 640, 512, 384, 256)
 LAYERS = 4
 CHUNKS = (256, 256, 512)
 PAIR = 2
+GROUPS = PAIR * sum(UNITS[1:]) // P
+FIRST = PAIR * UNITS[1] // P
+LAG = 3
 FLOPS = 2 * SAMPLES * TERMS * sum(UNITS[l] * UNITS[l + 1] for l in range(LAYERS))
 
 
@@ -26,7 +29,7 @@ def tile_mlp_cutoff_b_kernel(tc, x, w1, b1, w2, b2, w3, b3, w4, b4, offs, out):
 
     with (
         tc.tile_pool(name="held", bufs=1) as held,
-        tc.tile_pool(name="picked", bufs=PAIR * max(CHUNKS) // P) as picked,
+        tc.tile_pool(name="picked", bufs=4) as picked,
         tc.tile_pool(name="flipped", bufs=2 * PAIR) as flipped,
         tc.tile_pool(name="acts", bufs=2 * PAIR) as acts,
         tc.tile_pool(name="staged", bufs=4) as staged,
@@ -82,29 +85,39 @@ def tile_mlp_cutoff_b_kernel(tc, x, w1, b1, w2, b2, w3, b3, w4, b4, offs, out):
         bias = held.tile([P, bias_count], F32, name="bias")
         nc.vector.tensor_copy(bias[:], bias_ps[:])
 
-        def gather(start, width, terms):
-            rounded = {t: [] for t in terms}
-            for b in range(start // P, (start + width) // P):
-                for t in terms:
-                    piece = offsets[:, t * UNITS[0] // 16 : (t + 1) * UNITS[0] // 16]
-                    xi = picked.tile([P, UNITS[0]], F32, name="xi")
-                    nc.scalar.activation(xi[:], x_blocks[b][:].indirect(piece), COPY)
-                    xi_bf = picked.tile([P, UNITS[0]], BF16, name="xi_bf")
-                    nc.vector.tensor_copy(xi_bf[:], xi[:])
-                    rounded[t].append(xi_bf)
-            return rounded
+        rounded = {}
+        turn = {}
+        moving = {}
 
-        def flip(blocks):
-            width = len(blocks) * P
-            turn = turned.tile([P, k_tiles[0], width], BF16, name="turn")
-            for s, xi_bf in enumerate(blocks):
+        def prepare(job, g):
+            start, width, terms = job
+            blocks = width // P
+            units = [(t, s) for t in terms for s in range(blocks)]
+            every = (GROUPS - FIRST) // len(units)
+            u, rest = divmod(g - FIRST, every)
+            if rest == 0 and 0 <= u < len(units):
+                t, s = units[u]
+                piece = offsets[:, t * UNITS[0] // 16 : (t + 1) * UNITS[0] // 16]
+                xi = picked.tile([P, UNITS[0]], F32, name="xi")
+                nc.scalar.activation(xi[:], x_blocks[start // P + s][:].indirect(piece), COPY)
+                xi_bf = picked.tile([P, UNITS[0]], BF16, name="xi_bf")
+                nc.vector.tensor_copy(xi_bf[:], xi[:])
+                rounded[(t, s)] = xi_bf
+            u, rest = divmod(g - FIRST - LAG, every)
+            if rest == 0 and 0 <= u < len(units):
+                t, s = units[u]
+                if s == 0:
+                    turn[t] = turned.tile([P, k_tiles[0], width], BF16, name="turn")
                 for k in range(k_tiles[0]):
-                    nc.tensor.transpose(turn[:, k, s * P : (s + 1) * P], xi_bf[:, k * P : (k + 1) * P], ident_bf[:])
-            xi_t = flipped.tile([P, k_tiles[0], width], BF16, name="xi_t")
-            nc.vector.tensor_copy(xi_t[:], turn[:])
-            return [xi_t[:, k, :] for k in range(k_tiles[0])]
+                    nc.tensor.transpose(
+                        turn[t][:, k, s * P : (s + 1) * P], rounded[(t, s)][:, k * P : (k + 1) * P], ident_bf[:]
+                    )
+                if s == blocks - 1:
+                    xi_t = flipped.tile([P, k_tiles[0], width], BF16, name="xi_t")
+                    nc.vector.tensor_copy(xi_t[:], turn[t][:])
+                    moving[t] = [xi_t[:, k, :] for k in range(k_tiles[0])]
 
-        def dense(l, t, start, width, moving):
+        def dense(l, t, start, width, streamed, upcoming, g):
             last = l == LAYERS - 1
             h = None if last else acts.tile([P, m_tiles[l], width], BF16, name=f"h{l}")
             for m in range(m_tiles[l]):
@@ -113,7 +126,7 @@ def tile_mlp_cutoff_b_kernel(tc, x, w1, b1, w2, b2, w3, b3, w4, b4, offs, out):
                     nc.tensor.matmul(
                         acc[:],
                         weights[l][t][:, k, m * P : (m + 1) * P],
-                        moving[k],
+                        streamed[k],
                         start=(k == 0),
                         stop=(k == k_tiles[l] - 1),
                     )
@@ -127,6 +140,8 @@ def tile_mlp_cutoff_b_kernel(tc, x, w1, b1, w2, b2, w3, b3, w4, b4, offs, out):
                 if last:
                     row = t * UNITS[LAYERS] + m * P
                     nc.sync.dma_start(out[row : row + P, start : start + width], y[:])
+                if upcoming is not None:
+                    prepare(upcoming, g + m)
             return None if last else [h[:, m, :] for m in range(m_tiles[l])]
 
         jobs = [
@@ -134,13 +149,12 @@ def tile_mlp_cutoff_b_kernel(tc, x, w1, b1, w2, b2, w3, b3, w4, b4, offs, out):
             for c in range(len(CHUNKS))
             for first in range(0, TERMS, PAIR)
         ]
-        moving = {t: flip(blocks) for t, blocks in gather(*jobs[0]).items()}
+        for g in range(GROUPS):
+            prepare(jobs[0], g)
         for i, (start, width, terms) in enumerate(jobs):
+            upcoming = jobs[i + 1] if i + 1 < len(jobs) else None
+            g = 0
             for l in range(LAYERS):
                 for t in terms:
-                    moving[t] = dense(l, t, start, width, moving[t])
-                if i + 1 < len(jobs) and l == 0:
-                    rounded = gather(*jobs[i + 1])
-                if i + 1 < len(jobs) and l == 1:
-                    for t, blocks in rounded.items():
-                        moving[t] = flip(blocks)
+                    moving[t] = dense(l, t, start, width, moving[t], upcoming, g)
+                    g += m_tiles[l]

@@ -10,7 +10,7 @@ P = 128
 SAMPLES, FEATURES, ENTRIES, TERMS = 1024, 2048, 1024, 4
 UNITS = (256, 640, 512, 384, 256)
 LAYERS = 4
-CHUNKS = (256, 256, 512)
+CHUNKS = (256, 384, 384)
 PAIR = 2
 GROUPS = PAIR * sum(UNITS[1:]) // P
 FIRST = PAIR * UNITS[1] // P
@@ -29,7 +29,7 @@ def tile_mlp_cutoff_b_kernel(tc, x, w1, b1, w2, b2, w3, b3, w4, b4, offs, out):
 
     with (
         tc.tile_pool(name="held", bufs=1) as held,
-        tc.tile_pool(name="picked", bufs=4) as picked,
+        tc.tile_pool(name="picked", bufs=LAG + 2) as picked,
         tc.tile_pool(name="flipped", bufs=2 * PAIR) as flipped,
         tc.tile_pool(name="acts", bufs=2 * PAIR) as acts,
         tc.tile_pool(name="staged", bufs=4) as staged,
@@ -49,8 +49,8 @@ def tile_mlp_cutoff_b_kernel(tc, x, w1, b1, w2, b2, w3, b3, w4, b4, offs, out):
             for b in range(first, first + count):
                 nc.sync.dma_start(x_blocks[b][:], x[b * P : (b + 1) * P, :])
 
-        def load_weights(pair):
-            for l in range(LAYERS):
+        def load_weights(pair, layers):
+            for l in layers:
                 for t in range(pair * PAIR, (pair + 1) * PAIR):
                     nc.sync.dma_start(
                         weights[l][t][:],
@@ -66,9 +66,11 @@ def tile_mlp_cutoff_b_kernel(tc, x, w1, b1, w2, b2, w3, b3, w4, b4, offs, out):
                 b_dram[l].rearrange("(r p) one -> r (p one)", p=P),
             )
         load_x(1, CHUNKS[0] // P - 1)
-        load_weights(0)
-        load_weights(1)
-        load_x(CHUNKS[0] // P, (SAMPLES - CHUNKS[0]) // P)
+        load_weights(0, range(LAYERS))
+        load_weights(1, (0, 1))
+        load_x(CHUNKS[0] // P, CHUNKS[1] // P)
+        load_weights(1, (2, 3))
+        load_x((CHUNKS[0] + CHUNKS[1]) // P, CHUNKS[2] // P)
 
         zeros = held.tile([P, 1], F32, name="zeros")
         nc.vector.memset(zeros[:], 0.0)
@@ -86,36 +88,32 @@ def tile_mlp_cutoff_b_kernel(tc, x, w1, b1, w2, b2, w3, b3, w4, b4, offs, out):
         nc.vector.tensor_copy(bias[:], bias_ps[:])
 
         rounded = {}
-        turn = {}
         moving = {}
 
         def prepare(job, g):
             start, width, terms = job
-            blocks = width // P
-            units = [(t, s) for t in terms for s in range(blocks)]
-            every = (GROUPS - FIRST) // len(units)
+            units = [(s, t, k) for s in range(width // P) for t in terms for k in range(k_tiles[0])]
+            every = (GROUPS - FIRST - LAG) // len(units)
             u, rest = divmod(g - FIRST, every)
             if rest == 0 and 0 <= u < len(units):
-                t, s = units[u]
-                piece = offsets[:, t * UNITS[0] // 16 : (t + 1) * UNITS[0] // 16]
-                xi = picked.tile([P, UNITS[0]], F32, name="xi")
-                nc.scalar.activation(xi[:], x_blocks[start // P + s][:].indirect(piece), COPY)
-                xi_bf = picked.tile([P, UNITS[0]], BF16, name="xi_bf")
+                s, t, k = units[u]
+                entry = t * UNITS[0] + k * P
+                xi = picked.tile([P, P], F32, name="xi")
+                nc.scalar.activation(
+                    xi[:], x_blocks[start // P + s][:].indirect(offsets[:, entry // 16 : (entry + P) // 16]), COPY
+                )
+                xi_bf = picked.tile([P, P], BF16, name="xi_bf")
                 nc.vector.tensor_copy(xi_bf[:], xi[:])
-                rounded[(t, s)] = xi_bf
+                rounded[units[u]] = xi_bf
             u, rest = divmod(g - FIRST - LAG, every)
             if rest == 0 and 0 <= u < len(units):
-                t, s = units[u]
-                if s == 0:
-                    turn[t] = turned.tile([P, k_tiles[0], width], BF16, name="turn")
-                for k in range(k_tiles[0]):
-                    nc.tensor.transpose(
-                        turn[t][:, k, s * P : (s + 1) * P], rounded[(t, s)][:, k * P : (k + 1) * P], ident_bf[:]
-                    )
-                if s == blocks - 1:
+                s, t, k = units[u]
+                if s == 0 and k == 0:
                     xi_t = flipped.tile([P, k_tiles[0], width], BF16, name="xi_t")
-                    nc.vector.tensor_copy(xi_t[:], turn[t][:])
-                    moving[t] = [xi_t[:, k, :] for k in range(k_tiles[0])]
+                    moving[t] = [xi_t[:, j, :] for j in range(k_tiles[0])]
+                turn = turned.tile([P, P], BF16, name="turn")
+                nc.tensor.transpose(turn[:], rounded[units[u]][:], ident_bf[:])
+                nc.vector.tensor_copy(moving[t][k][:, s * P : (s + 1) * P], turn[:])
 
         def dense(l, t, start, width, streamed, upcoming, g):
             last = l == LAYERS - 1

@@ -33,8 +33,7 @@ def tile_mlp_cutoff_b_kernel(tc, x, w1, b1, w2, b2, w3, b3, w4, b4, offs, out):
         tc.tile_pool(name="flipped", bufs=2 * PAIR) as flipped,
         tc.tile_pool(name="acts", bufs=2 * PAIR) as acts,
         tc.tile_pool(name="staged", bufs=4) as staged,
-        tc.psum_pool(name="sums", bufs=6) as sums,
-        tc.psum_pool(name="turned", bufs=2) as turned,
+        tc.psum_pool(name="banks", bufs=8) as banks,
     ):
         offsets = held.tile([P, ENTRIES // 16], U16, name="offsets")
         nc.sync.dma_start(offsets[:], offs)
@@ -82,7 +81,7 @@ def tile_mlp_cutoff_b_kernel(tc, x, w1, b1, w2, b2, w3, b3, w4, b4, offs, out):
         ident_f = held.tile([bias_count, bias_count], F32, name="ident_f")
         make_identity(nc, ident_f[:])
 
-        bias_ps = sums.tile([P, bias_count], F32, name="acc")
+        bias_ps = banks.tile([P, bias_count], F32, name="bias_ps", tag="bank")
         nc.tensor.transpose(bias_ps[:], bias_rows[:], ident_f[:])
         bias = held.tile([P, bias_count], F32, name="bias")
         nc.vector.tensor_copy(bias[:], bias_ps[:])
@@ -111,7 +110,7 @@ def tile_mlp_cutoff_b_kernel(tc, x, w1, b1, w2, b2, w3, b3, w4, b4, offs, out):
                 if s == 0 and k == 0:
                     xi_t = flipped.tile([P, k_tiles[0], width], BF16, name="xi_t")
                     moving[t] = [xi_t[:, j, :] for j in range(k_tiles[0])]
-                turn = turned.tile([P, P], BF16, name="turn")
+                turn = banks.tile([P, P], BF16, name="turn", tag="bank")
                 nc.tensor.transpose(turn[:], rounded[units[u]][:], ident_bf[:])
                 nc.vector.tensor_copy(moving[t][k][:, s * P : (s + 1) * P], turn[:])
 
@@ -119,7 +118,7 @@ def tile_mlp_cutoff_b_kernel(tc, x, w1, b1, w2, b2, w3, b3, w4, b4, offs, out):
             last = l == LAYERS - 1
             h = None if last else acts.tile([P, m_tiles[l], width], BF16, name=f"h{l}")
             for m in range(m_tiles[l]):
-                acc = sums.tile([P, width], F32, name="acc")
+                acc = banks.tile([P, width], F32, name="acc", tag="bank")
                 for k in range(k_tiles[l]):
                     nc.tensor.matmul(
                         acc[:],

@@ -10,8 +10,8 @@ P = 128
 SAMPLES, FEATURES, ENTRIES, TERMS = 1024, 2048, 1024, 4
 UNITS = (256, 640, 512, 384, 256)
 LAYERS = 4
-CHUNKS = (256, 384, 384)
 PAIR = 2
+CHUNKS = ((256, 384, 384), (512, 512))
 GROUPS = PAIR * sum(UNITS[1:]) // P
 FIRST = PAIR * UNITS[1] // P
 LAG = 3
@@ -64,12 +64,14 @@ def tile_mlp_cutoff_b_kernel(tc, x, w1, b1, w2, b2, w3, b3, w4, b4, offs, out):
                 bias_rows[bias_base[l] : bias_base[l] + rows, :],
                 b_dram[l].rearrange("(r p) one -> r (p one)", p=P),
             )
-        load_x(1, CHUNKS[0] // P - 1)
-        load_weights(0, range(LAYERS))
-        load_weights(1, (0, 1))
-        load_x(CHUNKS[0] // P, CHUNKS[1] // P)
-        load_weights(1, (2, 3))
-        load_x((CHUNKS[0] + CHUNKS[1]) // P, CHUNKS[2] // P)
+        load_x(1, 1)
+        load_weights(0, (0, 1))
+        load_x(2, 1)
+        load_weights(0, (2,))
+        load_x(3, 1)
+        load_weights(0, (3,))
+        load_weights(1, range(LAYERS))
+        load_x(4, SAMPLES // P - 4)
 
         zeros = held.tile([P, 1], F32, name="zeros")
         nc.vector.memset(zeros[:], 0.0)
@@ -92,10 +94,8 @@ def tile_mlp_cutoff_b_kernel(tc, x, w1, b1, w2, b2, w3, b3, w4, b4, offs, out):
         def prepare(job, g):
             start, width, terms = job
             units = [(s, t, k) for s in range(width // P) for t in terms for k in range(k_tiles[0])]
-            every = (GROUPS - FIRST - LAG) // len(units)
-            u, rest = divmod(g - FIRST, every)
-            if rest == 0 and 0 <= u < len(units):
-                s, t, k = units[u]
+            span = GROUPS - FIRST - LAG
+            for s, t, k in [units[u] for u in range(len(units)) if u * span // len(units) == g - FIRST]:
                 entry = t * UNITS[0] + k * P
                 xi = picked.tile([P, P], F32, name="xi")
                 nc.scalar.activation(
@@ -103,15 +103,13 @@ def tile_mlp_cutoff_b_kernel(tc, x, w1, b1, w2, b2, w3, b3, w4, b4, offs, out):
                 )
                 xi_bf = picked.tile([P, P], BF16, name="xi_bf")
                 nc.vector.tensor_copy(xi_bf[:], xi[:])
-                rounded[units[u]] = xi_bf
-            u, rest = divmod(g - FIRST - LAG, every)
-            if rest == 0 and 0 <= u < len(units):
-                s, t, k = units[u]
+                rounded[(s, t, k)] = xi_bf
+            for s, t, k in [units[u] for u in range(len(units)) if u * span // len(units) == g - FIRST - LAG]:
                 if s == 0 and k == 0:
                     xi_t = flipped.tile([P, k_tiles[0], width], BF16, name="xi_t")
                     moving[t] = [xi_t[:, j, :] for j in range(k_tiles[0])]
                 turn = banks.tile([P, P], BF16, name="turn", tag="bank")
-                nc.tensor.transpose(turn[:], rounded[units[u]][:], ident_bf[:])
+                nc.tensor.transpose(turn[:], rounded[(s, t, k)][:], ident_bf[:])
                 nc.vector.tensor_copy(moving[t][k][:, s * P : (s + 1) * P], turn[:])
 
         def dense(l, t, start, width, streamed, upcoming, g):
@@ -142,9 +140,10 @@ def tile_mlp_cutoff_b_kernel(tc, x, w1, b1, w2, b2, w3, b3, w4, b4, offs, out):
             return None if last else [h[:, m, :] for m in range(m_tiles[l])]
 
         jobs = [
-            (sum(CHUNKS[:c]), CHUNKS[c], tuple(range(first, first + PAIR)))
-            for c in range(len(CHUNKS))
-            for first in range(0, TERMS, PAIR)
+            (sum(CHUNKS[pair][:c]), CHUNKS[pair][c], tuple(range(pair * PAIR, (pair + 1) * PAIR)))
+            for c in range(len(CHUNKS[0]))
+            for pair in range(TERMS // PAIR)
+            if c < len(CHUNKS[pair])
         ]
         for g in range(GROUPS):
             prepare(jobs[0], g)

import concourse.mybir as mybir
from concourse.masks import make_identity

BF16, F32, U16 = mybir.dt.bfloat16, mybir.dt.float32, mybir.dt.uint16
COPY = mybir.ActivationFunctionType.Copy
RELU = mybir.ActivationFunctionType.Relu
ADD, MAX = mybir.AluOpType.add, mybir.AluOpType.max

P = 128
SAMPLES, FEATURES, ENTRIES, TERMS = 1024, 2048, 1024, 4
UNITS = (256, 640, 512, 384, 256)
LAYERS = 4
PAIR = 2
CHUNKS = ((256, 384, 384), (512, 512))
GROUPS = PAIR * sum(UNITS[1:]) // P
FIRST = PAIR * UNITS[1] // P
LAG = 3
FLOPS = 2 * SAMPLES * TERMS * sum(UNITS[l] * UNITS[l + 1] for l in range(LAYERS))


def tile_mlp_cutoff_b_kernel(tc, x, w1, b1, w2, b2, w3, b3, w4, b4, offs, out):
    nc = tc.nc
    w_dram = (w1, w2, w3, w4)
    b_dram = (b1, b2, b3, b4)
    k_tiles = [UNITS[l] // P for l in range(LAYERS)]
    m_tiles = [UNITS[l + 1] // P for l in range(LAYERS)]
    bias_base = [TERMS * sum(m_tiles[:l]) for l in range(LAYERS)]
    bias_count = TERMS * sum(m_tiles)

    with (
        tc.tile_pool(name="held", bufs=1) as held,
        tc.tile_pool(name="picked", bufs=LAG + 2) as picked,
        tc.tile_pool(name="flipped", bufs=2 * PAIR) as flipped,
        tc.tile_pool(name="acts", bufs=2 * PAIR) as acts,
        tc.tile_pool(name="staged", bufs=4) as staged,
        tc.psum_pool(name="banks", bufs=8) as banks,
    ):
        offsets = held.tile([P, ENTRIES // 16], U16, name="offsets")
        nc.sync.dma_start(offsets[:], offs)

        x_blocks = [held.tile([P, FEATURES], F32, name=f"x{b}") for b in range(SAMPLES // P)]
        weights = [
            [held.tile([P, k_tiles[l], UNITS[l + 1]], BF16, name=f"w{l}_{t}") for t in range(TERMS)]
            for l in range(LAYERS)
        ]

        def load_x(first, count):
            for b in range(first, first + count):
                nc.sync.dma_start(x_blocks[b][:], x[b * P : (b + 1) * P, :])

        def load_weights(pair, layers):
            for l in layers:
                for t in range(pair * PAIR, (pair + 1) * PAIR):
                    nc.sync.dma_start(
                        weights[l][t][:],
                        w_dram[l][t * UNITS[l] : (t + 1) * UNITS[l], :].rearrange("(k p) a -> p k a", p=P),
                    )

        load_x(0, 1)
        bias_rows = held.tile([bias_count, P], F32, name="bias_rows")
        for l in range(LAYERS):
            rows = TERMS * m_tiles[l]
            nc.sync.dma_start(
                bias_rows[bias_base[l] : bias_base[l] + rows, :],
                b_dram[l].rearrange("(r p) one -> r (p one)", p=P),
            )
        load_x(1, 1)
        load_weights(0, (0, 1))
        load_x(2, 1)
        load_weights(0, (2,))
        load_x(3, 1)
        load_weights(0, (3,))
        load_weights(1, range(LAYERS))
        load_x(4, SAMPLES // P - 4)

        zeros = held.tile([P, 1], F32, name="zeros")
        nc.vector.memset(zeros[:], 0.0)
        primed = held.tile([P, 1], F32, name="primed")
        nc.scalar.activation(primed[:], zeros[:], COPY)

        ident_bf = held.tile([P, P], BF16, name="ident_bf")
        make_identity(nc, ident_bf[:])
        ident_f = held.tile([bias_count, bias_count], F32, name="ident_f")
        make_identity(nc, ident_f[:])

        bias_ps = banks.tile([P, bias_count], F32, name="bias_ps", tag="bank")
        nc.tensor.transpose(bias_ps[:], bias_rows[:], ident_f[:])
        bias = held.tile([P, bias_count], F32, name="bias")
        nc.vector.tensor_copy(bias[:], bias_ps[:])

        rounded = {}
        moving = {}

        def prepare(job, g):
            start, width, terms = job
            units = [(s, t, k) for s in range(width // P) for t in terms for k in range(k_tiles[0])]
            span = GROUPS - FIRST - LAG
            for s, t, k in [units[u] for u in range(len(units)) if u * span // len(units) == g - FIRST]:
                entry = t * UNITS[0] + k * P
                xi = picked.tile([P, P], F32, name="xi")
                nc.scalar.activation(
                    xi[:], x_blocks[start // P + s][:].indirect(offsets[:, entry // 16 : (entry + P) // 16]), COPY
                )
                xi_bf = picked.tile([P, P], BF16, name="xi_bf")
                nc.vector.tensor_copy(xi_bf[:], xi[:])
                rounded[(s, t, k)] = xi_bf
            for s, t, k in [units[u] for u in range(len(units)) if u * span // len(units) == g - FIRST - LAG]:
                if s == 0 and k == 0:
                    xi_t = flipped.tile([P, k_tiles[0], width], BF16, name="xi_t")
                    moving[t] = [xi_t[:, j, :] for j in range(k_tiles[0])]
                turn = banks.tile([P, P], BF16, name="turn", tag="bank")
                nc.tensor.transpose(turn[:], rounded[(s, t, k)][:], ident_bf[:])
                nc.vector.tensor_copy(moving[t][k][:, s * P : (s + 1) * P], turn[:])

        def dense(l, t, start, width, streamed, upcoming, g):
            last = l == LAYERS - 1
            h = None if last else acts.tile([P, m_tiles[l], width], BF16, name=f"h{l}")
            for m in range(m_tiles[l]):
                acc = banks.tile([P, width], F32, name="acc", tag="bank")
                for k in range(k_tiles[l]):
                    nc.tensor.matmul(
                        acc[:],
                        weights[l][t][:, k, m * P : (m + 1) * P],
                        streamed[k],
                        start=(k == 0),
                        stop=(k == k_tiles[l] - 1),
                    )
                column = bias_base[l] + t * m_tiles[l] + m
                y = staged.tile([P, width], F32, name="y") if last else None
                dest = y[:] if last else h[:, m, :]
                if m % 2 == 0:
                    nc.vector.tensor_scalar(dest, acc[:], bias[:, column : column + 1], 0.0, ADD, MAX)
                else:
                    nc.scalar.activation(dest, acc[:], RELU, bias=bias[:, column : column + 1])
                if last:
                    row = t * UNITS[LAYERS] + m * P
                    nc.sync.dma_start(out[row : row + P, start : start + width], y[:])
                if upcoming is not None:
                    prepare(upcoming, g + m)
            return None if last else [h[:, m, :] for m in range(m_tiles[l])]

        jobs = [
            (sum(CHUNKS[pair][:c]), CHUNKS[pair][c], tuple(range(pair * PAIR, (pair + 1) * PAIR)))
            for c in range(len(CHUNKS[0]))
            for pair in range(TERMS // PAIR)
            if c < len(CHUNKS[pair])
        ]
        for g in range(GROUPS):
            prepare(jobs[0], g)
        for i, (start, width, terms) in enumerate(jobs):
            upcoming = jobs[i + 1] if i + 1 < len(jobs) else None
            g = 0
            for l in range(LAYERS):
                for t in terms:
                    moving[t] = dense(l, t, start, width, moving[t], upcoming, g)
                    g += m_tiles[l]
